import numpy as np
import ml_dtypes


def mxq(x, axis, fmt="e4m3"):
    dtype, down = {"e4m3": (ml_dtypes.float8_e4m3fn, 7), "e5m2": (ml_dtypes.float8_e5m2, 14)}[fmt]
    v = np.moveaxis(np.asarray(x, np.float32).astype(ml_dtypes.bfloat16).astype(np.float64), axis, -1)
    blocks = v.reshape(v.shape[:-1] + (-1, 32))
    amax = np.abs(blocks).max(-1, keepdims=True)
    byte = np.maximum(np.where(amax > 0, np.frexp(amax)[1] - 1 + 127, 0) - down, 1)
    scale = np.exp2(byte - 127.0)
    codes = (blocks / scale).astype(np.float32).astype(dtype).astype(np.float64)
    return np.moveaxis((codes * scale).reshape(v.shape), -1, axis)


WIDE = False


def mx_kscale(k):
    if not WIDE:
        return np.ones(k)
    levels = np.array([10, -10, 5, -5, 0])
    a = np.random.permutation(np.resize(levels, k // 512 * 4)).reshape(k // 512, 4)
    idx = np.arange(k)
    return np.exp2(a[idx // 512, idx % 128 // 32])


BF16 = ml_dtypes.bfloat16


def bf(x):
    return np.asarray(x, np.float32).astype(BF16)


def f64(x):
    return np.asarray(x).astype(np.float64)


E2M1 = np.array([0.0, 0.5, 1.0, 1.5, 2.0, 3.0, 4.0, 6.0, -0.0, -0.5, -1.0, -1.5, -2.0, -3.0, -4.0, -6.0])


def pack_weight(w, fmt):
    k, n = w.shape
    w = f64(bf(w)).reshape(k // 32, 32, n)
    amax = np.abs(w).max(1)
    if fmt == "e4m3":
        byte = np.frexp(amax)[1] - 1 + 127 - 7
    else:
        mant, ex = np.frexp(amax / 6.0)
        byte = np.where(mant > 0.5, ex, ex - 1) + 127
    byte = np.clip(np.where(amax > 0, byte, 1), 1, 254)
    scaled = (w * np.exp2(127.0 - byte)[:, None, :]).reshape(k, n).astype(np.float32)
    by_word = np.ascontiguousarray(scaled.reshape(k // 512, 128, 4, n).transpose(0, 1, 3, 2))
    if fmt == "e4m3":
        words = by_word.astype(ml_dtypes.float8_e4m3fn).view(np.uint8)
    else:
        c = by_word.astype(ml_dtypes.float4_e2m1fn).view(np.uint8) & 0xF
        words = c[..., 0::2] | (c[..., 1::2] << 4)
    return np.ascontiguousarray(words), np.ascontiguousarray(byte.astype(np.uint8).reshape(k // 512, 16, n))


def unpack_weight(words, scales, fmt):
    g, p, n, _ = words.shape
    if fmt == "e4m3":
        vals = np.ascontiguousarray(words).view(ml_dtypes.float8_e4m3fn).astype(np.float64)
    else:
        nib = np.empty((g, p, n, 4), np.uint8)
        nib[..., 0::2] = words & 0xF
        nib[..., 1::2] = words >> 4
        vals = E2M1[nib]
    vals = vals * np.repeat(np.exp2(scales.astype(np.float64) - 127.0), 8, axis=1)[..., None]
    return vals.transpose(0, 1, 3, 2).reshape(g * 512, n)

def pack4(w):
    words, scales = pack_weight(w, "e2m1")
    return words.reshape(words.shape[0], 128, -1), scales


def unpack4(words, scales):
    return unpack_weight(words.reshape(words.shape[0], 128, -1, 2), scales, "e2m1")


B, L, C, H, BLK = 2, 128, 512, 16, 128
D = C // H
MAX_SCALE_MUL = np.log(100.0)
EPS = 1e-12


def l2norm(t):
    n = np.sqrt(np.sum(t * t, axis=-1, keepdims=True))
    return t / np.maximum(n, EPS)


def setup_inputs():
    s = mx_kscale(C)
    lsm = np.linspace(np.log(4.0), MAX_SCALE_MUL + 1.0, H) + 0.05 * np.random.standard_normal(H)
    x = bf(np.random.standard_normal((B, L, C)) * s)
    w = np.random.standard_normal((3 * C, C)) / np.sqrt(C) / s[None, :]
    words, scales = pack4(np.ascontiguousarray(w.T))
    q_bias = bf(np.random.standard_normal(C) * 0.3)
    v_bias = bf(np.random.standard_normal(C) * 0.3)
    return {"x": x,
            "W_qkv_words": words,
            "W_qkv_scales": scales,
            "q_bias": q_bias,
            "v_bias": v_bias,
            "log_scale_mul": bf(lsm.reshape(1, H, 1, 1))}


def reference(x, W_qkv_words, W_qkv_scales, q_bias, v_bias, log_scale_mul):
    qb = f64(q_bias)
    bias = np.concatenate([qb, np.zeros_like(qb), f64(v_bias)])
    qkv = (mxq(f64(x), 2, "e4m3") @ unpack4(W_qkv_words, W_qkv_scales)) + bias
    qkv = qkv.reshape(B, L, 3, H, D)
    q, k, v = np.moveaxis(qkv, 2, 0)
    q = np.swapaxes(q, 1, 2)
    k = np.swapaxes(k, 1, 2)
    v = np.swapaxes(v, 1, 2)
    scale_mul = np.exp(np.minimum(f64(log_scale_mul), MAX_SCALE_MUL))
    q = l2norm(q) * scale_mul
    k = l2norm(k)
    return q, k, v

@@ -1,0 +1,167 @@
+import math
+from contextlib import ExitStack
+
+import concourse.mybir as mybir
+from concourse.masks import make_identity
+
+F32 = mybir.dt.float32
+BF16 = mybir.dt.bfloat16
+I32 = mybir.dt.int32
+U32 = mybir.dt.uint32
+U8 = mybir.dt.uint8
+FP8X4 = mybir.dt.float8_e4m3fn_x4
+FP4X4 = mybir.dt.float4_e2m1fn_x4
+ACT = mybir.ActivationFunctionType
+ALU = mybir.AluOpType
+AX = mybir.AxisListType
+
+P = 128
+B, L, C, H, D = 2, 128, 512, 16, 32
+PACK = 4
+TILES = C // P
+HEADS_PER_TILE = P // D
+RUN = L // D
+SEGS = TILES * RUN
+MAX_LOG_MUL = math.log(100.0)
+EPS = 1e-12
+
+FLOPS = 2 * B * L * C * 3 * C
+
+
+def tile_selfattention_pa_s_kernel(
+    tc, x, W_qkv_words, W_qkv_scales, q_bias, v_bias, log_scale_mul, out_0, out_1, out_2
+):
+    nc = tc.nc
+    with ExitStack() as ctx:
+        const = ctx.enter_context(tc.tile_pool(name="const", bufs=1))
+        work = ctx.enter_context(tc.tile_pool(name="work", bufs=6))
+        xt_pool = ctx.enter_context(tc.psum_pool(name="xt_pool", bufs=2))
+        bias_pool = ctx.enter_context(tc.psum_pool(name="bias_pool", bufs=1))
+        acc_pool = ctx.enter_context(tc.psum_pool(name="acc_pool", bufs=5))
+
+        x_sb = const.tile([P, B, C], BF16)
+        nc.sync.dma_start(out=x_sb[:], in_=x.rearrange("b l c -> l b c"))
+
+        w_scales = const.tile([P, 3 * C], U8, align_bytes=64)
+        nc.vector.memset(w_scales[:].bitcast(I32), 0)
+        for quad in range(4):
+            nc.sync.dma_start(
+                out=w_scales[32 * quad : 32 * quad + 4, :].bitcast(I32),
+                in_=W_qkv_scales[0, 4 * quad : 4 * quad + 4, :].bitcast(I32),
+            )
+        w_words = const.tile([P, 2 * 3 * C], U8, align_bytes=64)
+        nc.sync.dma_start(out=w_words[:].bitcast(I32), in_=W_qkv_words[0].bitcast(I32))
+
+        bias_rows = const.tile([P, P], BF16)
+        nc.vector.memset(bias_rows[:], 0.0)
+        nc.scalar.dma_start(out=bias_rows[0:TILES, :], in_=q_bias.rearrange("(f n) -> f n", n=P))
+        nc.scalar.dma_start(
+            out=bias_rows[TILES : 2 * TILES, :], in_=v_bias.rearrange("(f n) -> f n", n=P)
+        )
+        log_mul_all = const.tile([P, H], BF16)
+        nc.scalar.dma_start(
+            out=log_mul_all[:],
+            in_=log_scale_mul.rearrange("o h p q -> (o h p q)").partition_broadcast(P),
+        )
+
+        ident = const.tile([P, P], F32)
+        make_identity(nc, ident[:])
+
+        grouped = const.tile([P, B, L * PACK], BF16, align_bytes=64)
+        x_codes = const.tile([P, B, L], U32, align_bytes=64)
+        x_scales = const.tile([P, B, L], U8, align_bytes=64)
+        for b in range(B):
+            x_words = x_sb[:, b, :].bitcast(F32)
+            xt = xt_pool.tile([P, 2, L], F32)
+            for u in range(2):
+                nc.tensor.transpose(xt[:, u, :], x_words[:, u : C // 2 : 2], ident[:])
+            nc.vector.tensor_copy(
+                out=grouped[:, b, :].bitcast(F32).rearrange("p (j a u) -> p j a u", j=RUN, u=2),
+                in_=xt[:].rearrange("p u (a j) -> p j a u", j=RUN),
+            )
+        for b in range(B):
+            nc.vector.quantize_mx(
+                out=x_codes[:, b, :].bitcast(FP8X4), scales=x_scales[:, b, :], in_=grouped[:, b, :]
+            )
+
+        bias_rows_f32 = const.tile([P, P], F32)
+        nc.vector.tensor_copy(out=bias_rows_f32[:], in_=bias_rows[:])
+        bias_t = bias_pool.tile([P, P], F32)
+        nc.tensor.transpose(bias_t[:], bias_rows_f32[:], ident[:])
+        bias_col = const.tile([P, 2 * TILES], F32)
+        nc.vector.tensor_copy(out=bias_col[:], in_=bias_t[:, 0 : 2 * TILES])
+
+        log_mul = const.tile([P, TILES], F32)
+        for i in range(HEADS_PER_TILE):
+            rows = slice(D * i, D * (i + 1))
+            nc.vector.tensor_scalar_min(
+                out=log_mul[rows, :], in0=log_mul_all[rows, i:H:HEADS_PER_TILE], scalar1=MAX_LOG_MUL
+            )
+        scale_mul = const.tile([P, TILES], F32)
+        nc.scalar.activation(out=scale_mul[:], in_=log_mul[:], func=ACT.Exp)
+        table_warm = const.tile([P, TILES], F32)
+        nc.scalar.activation(out=table_warm[:], in_=scale_mul[:], func=ACT.Sqrt)
+
+        for b in range(B):
+            for part in ("k", "q", "v"):
+                first_tile = {"q": 0, "k": TILES, "v": 2 * TILES}[part]
+                dst = {"q": out_0, "k": out_1, "v": out_2}[part]
+                bias_at = {"q": 0, "k": None, "v": TILES}[part]
+
+                acc = acc_pool.tile([P, TILES, L], F32)
+                for f in range(TILES):
+                    t = first_tile + f
+                    nc.tensor.matmul_mx(
+                        out=acc[:, f, :],
+                        lhsT=w_words[:, 2 * P * t : 2 * P * (t + 1)].bitcast(FP4X4),
+                        lhsT_scale=w_scales[:, P * t : P * (t + 1)],
+                        rhs=x_codes[:, b, :].bitcast(FP8X4),
+                        rhs_scale=x_scales[:, b, :],
+                        start=True,
+                        stop=True,
+                    )
+                raw = acc
+                if bias_at is not None:
+                    raw = work.tile([P, TILES, L], F32, name="biased", align_bytes=64)
+                    for f in range(TILES):
+                        nc.scalar.activation(
+                            out=raw[:, f, :],
+                            in_=acc[:, f, :],
+                            func=ACT.Identity,
+                            bias=bias_col[:, bias_at + f : bias_at + f + 1],
+                            scale=1.0,
+                        )
+
+                heads = work.tile([P, SEGS, D], F32, align_bytes=64)
+                nc.vector.transpose(
+                    out=heads[:].rearrange("p s d -> p (s d)"), in_=raw[:].rearrange("p f n -> p (f n)")
+                )
+                result = heads
+                if part != "v":
+                    squares = work.tile([P, SEGS, D], F32)
+                    nc.scalar.activation(out=squares[:], in_=heads[:], func=ACT.Square)
+                    sumsq = work.tile([P, SEGS], F32)
+                    nc.vector.tensor_reduce(out=sumsq[:], in_=squares[:], axis=AX.X, op=ALU.add)
+                    nc.vector.tensor_scalar_max(out=sumsq[:], in0=sumsq[:], scalar1=EPS * EPS)
+                    inv_sumsq = work.tile([P, SEGS], F32)
+                    nc.vector.reciprocal(out=inv_sumsq[:], in_=sumsq[:])
+                    factor = work.tile([P, TILES, RUN], F32)
+                    nc.scalar.activation(
+                        out=factor[:].rearrange("p f j -> p (f j)"), in_=inv_sumsq[:], func=ACT.Sqrt
+                    )
+                    if part == "q":
+                        nc.vector.tensor_mul(
+                            out=factor[:],
+                            in0=factor[:],
+                            in1=scale_mul[:].unsqueeze(2).to_broadcast([P, TILES, RUN]),
+                        )
+                    result = work.tile([P, SEGS, D], F32)
+                    nc.vector.tensor_mul(
+                        out=result[:],
+                        in0=heads[:],
+                        in1=factor[:].rearrange("p f j -> p (f j)").unsqueeze(2).to_broadcast([P, SEGS, D]),
+                    )
+                nc.sync.dma_start(
+                    out=dst[b].rearrange("(f i) (a j) d -> (i a) f (j d)", i=HEADS_PER_TILE, j=RUN),
+                    in_=result[:].rearrange("p (f j) d -> p f (j d)", j=RUN),
+                )

@@ -1,4 +1,3 @@
-import math
 from contextlib import ExitStack
 
 import concourse.mybir as mybir
@@ -22,7 +21,7 @@ TILES = C // P
 HEADS_PER_TILE = P // D
 RUN = L // D
 SEGS = TILES * RUN
-MAX_LOG_MUL = math.log(100.0)
+MAX_MUL = 100.0
 EPS = 1e-12
 
 FLOPS = 2 * B * L * C * 3 * C
@@ -32,40 +31,63 @@ def tile_selfattention_pa_s_kernel(
     tc, x, W_qkv_words, W_qkv_scales, q_bias, v_bias, log_scale_mul, out_0, out_1, out_2
 ):
     nc = tc.nc
+    outputs = {"q": out_0, "k": out_1, "v": out_2}
+    first_tile = {"q": 0, "k": TILES, "v": 2 * TILES}
+    bias_column = {"q": 0, "v": TILES}
+
     with ExitStack() as ctx:
         const = ctx.enter_context(tc.tile_pool(name="const", bufs=1))
         work = ctx.enter_context(tc.tile_pool(name="work", bufs=6))
         xt_pool = ctx.enter_context(tc.psum_pool(name="xt_pool", bufs=2))
         bias_pool = ctx.enter_context(tc.psum_pool(name="bias_pool", bufs=1))
         acc_pool = ctx.enter_context(tc.psum_pool(name="acc_pool", bufs=5))
-
-        x_sb = const.tile([P, B, C], BF16)
-        nc.sync.dma_start(out=x_sb[:], in_=x.rearrange("b l c -> l b c"))
+        ctx.enter_context(tc.manual_schedule())
 
         w_scales = const.tile([P, 3 * C], U8, align_bytes=64)
-        nc.vector.memset(w_scales[:].bitcast(I32), 0)
+        nc.gpsimd.memset(w_scales[:].bitcast(F32), 0.0)
+        bias_rows = const.tile([P, P], BF16)
+        nc.gpsimd.memset(bias_rows[:], 0.0)
+
+        x_sb = const.tile([P, B, C], BF16)
+        for b in range(B):
+            nc.sync.dma_start(out=x_sb[:, b, :], in_=x[b])
+        w_words = const.tile([P, 2 * 3 * C], U8, align_bytes=64)
+        nc.sync.dma_start(out=w_words[:].bitcast(I32), in_=W_qkv_words[0].bitcast(I32))
         for quad in range(4):
             nc.sync.dma_start(
                 out=w_scales[32 * quad : 32 * quad + 4, :].bitcast(I32),
                 in_=W_qkv_scales[0, 4 * quad : 4 * quad + 4, :].bitcast(I32),
             )
-        w_words = const.tile([P, 2 * 3 * C], U8, align_bytes=64)
-        nc.sync.dma_start(out=w_words[:].bitcast(I32), in_=W_qkv_words[0].bitcast(I32))
 
-        bias_rows = const.tile([P, P], BF16)
-        nc.vector.memset(bias_rows[:], 0.0)
-        nc.scalar.dma_start(out=bias_rows[0:TILES, :], in_=q_bias.rearrange("(f n) -> f n", n=P))
-        nc.scalar.dma_start(
-            out=bias_rows[TILES : 2 * TILES, :], in_=v_bias.rearrange("(f n) -> f n", n=P)
-        )
         log_mul_all = const.tile([P, H], BF16)
         nc.scalar.dma_start(
             out=log_mul_all[:],
             in_=log_scale_mul.rearrange("o h p q -> (o h p q)").partition_broadcast(P),
         )
+        nc.scalar.dma_start(out=bias_rows[0:TILES, :], in_=q_bias.rearrange("(f n) -> f n", n=P))
+        nc.scalar.dma_start(
+            out=bias_rows[TILES : 2 * TILES, :], in_=v_bias.rearrange("(f n) -> f n", n=P)
+        )
 
         ident = const.tile([P, P], F32)
         make_identity(nc, ident[:])
+        ident_bf16 = const.tile([P, P], BF16)
+        make_identity(nc, ident_bf16[:])
+
+        mul_all = const.tile([P, H], F32)
+        nc.scalar.activation(out=mul_all[:], in_=log_mul_all[:], func=ACT.Exp)
+        table_warm = const.tile([P, H], F32)
+        nc.scalar.activation(out=table_warm[:], in_=mul_all[:], func=ACT.Abs_reciprocal_sqrt)
+        floor = const.tile([P, 1], F32)
+        nc.gpsimd.memset(floor[:], EPS * EPS)
+        neg_floor = const.tile([P, 1], F32)
+        nc.gpsimd.memset(neg_floor[:], -EPS * EPS)
+        scale_mul = const.tile([P, TILES], F32)
+        for i in range(HEADS_PER_TILE):
+            rows = slice(D * i, D * (i + 1))
+            nc.gpsimd.tensor_scalar_min(
+                out=scale_mul[rows, :], in0=mul_all[rows, i:H:HEADS_PER_TILE], scalar1=MAX_MUL
+            )
 
         grouped = const.tile([P, B, L * PACK], BF16, align_bytes=64)
         x_codes = const.tile([P, B, L], U32, align_bytes=64)
@@ -79,89 +101,128 @@ def tile_selfattention_pa_s_kernel(
                 out=grouped[:, b, :].bitcast(F32).rearrange("p (j a u) -> p j a u", j=RUN, u=2),
                 in_=xt[:].rearrange("p u (a j) -> p j a u", j=RUN),
             )
-        for b in range(B):
             nc.vector.quantize_mx(
                 out=x_codes[:, b, :].bitcast(FP8X4), scales=x_scales[:, b, :], in_=grouped[:, b, :]
             )
 
-        bias_rows_f32 = const.tile([P, P], F32)
-        nc.vector.tensor_copy(out=bias_rows_f32[:], in_=bias_rows[:])
-        bias_t = bias_pool.tile([P, P], F32)
-        nc.tensor.transpose(bias_t[:], bias_rows_f32[:], ident[:])
+        bias_t = bias_pool.tile([P, P], BF16)
+        nc.tensor.transpose(bias_t[:], bias_rows[:], ident_bf16[:])
         bias_col = const.tile([P, 2 * TILES], F32)
         nc.vector.tensor_copy(out=bias_col[:], in_=bias_t[:, 0 : 2 * TILES])
 
-        log_mul = const.tile([P, TILES], F32)
-        for i in range(HEADS_PER_TILE):
-            rows = slice(D * i, D * (i + 1))
-            nc.vector.tensor_scalar_min(
-                out=log_mul[rows, :], in0=log_mul_all[rows, i:H:HEADS_PER_TILE], scalar1=MAX_LOG_MUL
+        raw = {}
+        heads = {}
+        squares = {}
+        factor = {}
+
+        def project(part, b):
+            acc = acc_pool.tile([P, TILES, L], F32)
+            for f in range(TILES):
+                t = first_tile[part] + f
+                nc.tensor.matmul_mx(
+                    out=acc[:, f, :],
+                    lhsT=w_words[:, 2 * P * t : 2 * P * (t + 1)].bitcast(FP4X4),
+                    lhsT_scale=w_scales[:, P * t : P * (t + 1)],
+                    rhs=x_codes[:, b, :].bitcast(FP8X4),
+                    rhs_scale=x_scales[:, b, :],
+                    start=True,
+                    stop=True,
+                )
+            raw[part, b] = acc
+
+        def add_bias(part, b):
+            biased = work.tile([P, TILES, L], F32, align_bytes=64)
+            for f in range(TILES):
+                column = bias_column[part] + f
+                nc.scalar.activation(
+                    out=biased[:, f, :],
+                    in_=raw[part, b][:, f, :],
+                    func=ACT.Identity,
+                    bias=bias_col[:, column : column + 1],
+                    scale=1.0,
+                )
+            raw[part, b] = biased
+
+        def turn(part, b):
+            turned = work.tile([P, SEGS, D], F32, align_bytes=64)
+            nc.vector.transpose(
+                out=turned[:].rearrange("p s d -> p (s d)"),
+                in_=raw[part, b][:].rearrange("p f n -> p (f n)"),
             )
-        scale_mul = const.tile([P, TILES], F32)
-        nc.scalar.activation(out=scale_mul[:], in_=log_mul[:], func=ACT.Exp)
-        table_warm = const.tile([P, TILES], F32)
-        nc.scalar.activation(out=table_warm[:], in_=scale_mul[:], func=ACT.Sqrt)
+            heads[part, b] = turned
+
+        def square(part, b):
+            squared = work.tile([P, SEGS, D], F32)
+            nc.scalar.activation(out=squared[:], in_=heads[part, b][:], func=ACT.Square)
+            squares[part, b] = squared
+
+        def sum_squares(part, b):
+            sumsq = work.tile([P, SEGS], F32)
+            nc.vector.tensor_reduce(out=sumsq[:], in_=squares[part, b][:], axis=AX.X, op=ALU.add)
+            squares[part, b] = sumsq
+
+        def inverse_norm(part, b):
+            excess = work.tile([P, SEGS], F32)
+            nc.scalar.activation(
+                out=excess[:], in_=squares[part, b][:], func=ACT.Relu, bias=neg_floor[:], scale=1.0
+            )
+            inv_norm = work.tile([P, TILES, RUN], F32)
+            nc.scalar.activation(
+                out=inv_norm[:].rearrange("p f j -> p (f j)"),
+                in_=excess[:],
+                func=ACT.Abs_reciprocal_sqrt,
+                bias=floor[:],
+                scale=1.0,
+            )
+            factor[part, b] = inv_norm
+
+        def scale(part, b):
+            if part == "q":
+                nc.vector.tensor_mul(
+                    out=factor[part, b][:],
+                    in0=factor[part, b][:],
+                    in1=scale_mul[:].unsqueeze(2).to_broadcast([P, TILES, RUN]),
+                )
+            scaled = work.tile([P, SEGS, D], F32)
+            nc.vector.tensor_mul(
+                out=scaled[:],
+                in0=heads[part, b][:],
+                in1=factor[part, b][:]
+                .rearrange("p f j -> p (f j)")
+                .unsqueeze(2)
+                .to_broadcast([P, SEGS, D]),
+            )
+            heads[part, b] = scaled
+
+        def store(part, b):
+            nc.sync.dma_start(
+                out=outputs[part][b].rearrange(
+                    "(f i) (a j) d -> (i a) f (j d)", i=HEADS_PER_TILE, j=RUN
+                ),
+                in_=heads[part, b][:].rearrange("p (f j) d -> p f (j d)", j=RUN),
+            )
 
         for b in range(B):
-            for part in ("k", "q", "v"):
-                first_tile = {"q": 0, "k": TILES, "v": 2 * TILES}[part]
-                dst = {"q": out_0, "k": out_1, "v": out_2}[part]
-                bias_at = {"q": 0, "k": None, "v": TILES}[part]
-
-                acc = acc_pool.tile([P, TILES, L], F32)
-                for f in range(TILES):
-                    t = first_tile + f
-                    nc.tensor.matmul_mx(
-                        out=acc[:, f, :],
-                        lhsT=w_words[:, 2 * P * t : 2 * P * (t + 1)].bitcast(FP4X4),
-                        lhsT_scale=w_scales[:, P * t : P * (t + 1)],
-                        rhs=x_codes[:, b, :].bitcast(FP8X4),
-                        rhs_scale=x_scales[:, b, :],
-                        start=True,
-                        stop=True,
-                    )
-                raw = acc
-                if bias_at is not None:
-                    raw = work.tile([P, TILES, L], F32, name="biased", align_bytes=64)
-                    for f in range(TILES):
-                        nc.scalar.activation(
-                            out=raw[:, f, :],
-                            in_=acc[:, f, :],
-                            func=ACT.Identity,
-                            bias=bias_col[:, bias_at + f : bias_at + f + 1],
-                            scale=1.0,
-                        )
-
-                heads = work.tile([P, SEGS, D], F32, align_bytes=64)
-                nc.vector.transpose(
-                    out=heads[:].rearrange("p s d -> p (s d)"), in_=raw[:].rearrange("p f n -> p (f n)")
-                )
-                result = heads
-                if part != "v":
-                    squares = work.tile([P, SEGS, D], F32)
-                    nc.scalar.activation(out=squares[:], in_=heads[:], func=ACT.Square)
-                    sumsq = work.tile([P, SEGS], F32)
-                    nc.vector.tensor_reduce(out=sumsq[:], in_=squares[:], axis=AX.X, op=ALU.add)
-                    nc.vector.tensor_scalar_max(out=sumsq[:], in0=sumsq[:], scalar1=EPS * EPS)
-                    inv_sumsq = work.tile([P, SEGS], F32)
-                    nc.vector.reciprocal(out=inv_sumsq[:], in_=sumsq[:])
-                    factor = work.tile([P, TILES, RUN], F32)
-                    nc.scalar.activation(
-                        out=factor[:].rearrange("p f j -> p (f j)"), in_=inv_sumsq[:], func=ACT.Sqrt
-                    )
-                    if part == "q":
-                        nc.vector.tensor_mul(
-                            out=factor[:],
-                            in0=factor[:],
-                            in1=scale_mul[:].unsqueeze(2).to_broadcast([P, TILES, RUN]),
-                        )
-                    result = work.tile([P, SEGS, D], F32)
-                    nc.vector.tensor_mul(
-                        out=result[:],
-                        in0=heads[:],
-                        in1=factor[:].rearrange("p f j -> p (f j)").unsqueeze(2).to_broadcast([P, SEGS, D]),
-                    )
-                nc.sync.dma_start(
-                    out=dst[b].rearrange("(f i) (a j) d -> (i a) f (j d)", i=HEADS_PER_TILE, j=RUN),
-                    in_=result[:].rearrange("p (f j) d -> p f (j d)", j=RUN),
-                )
+            project("q", b)
+            add_bias("q", b)
+            project("k", b)
+        for b in range(B):
+            turn("k", b)
+            turn("q", b)
+        for b in range(B):
+            project("v", b)
+            square("k", b)
+            square("q", b)
+            add_bias("v", b)
+        for b in range(B):
+            sum_squares("k", b)
+            sum_squares("q", b)
+            turn("v", b)
+            store("v", b)
+        for b in range(B):
+            inverse_norm("k", b)
+            inverse_norm("q", b)
+        for b in range(B):
+            for part in ("k", "q"):
+                scale(part, b)
+                store(part, b)

@@ -1,3 +1,4 @@
+import math
 from contextlib import ExitStack
 
 import concourse.mybir as mybir
@@ -43,14 +44,15 @@ def tile_selfattention_pa_s_kernel(
         acc_pool = ctx.enter_context(tc.psum_pool(name="acc_pool", bufs=5))
         ctx.enter_context(tc.manual_schedule())
 
-        w_scales = const.tile([P, 3 * C], U8, align_bytes=64)
-        nc.gpsimd.memset(w_scales[:].bitcast(F32), 0.0)
         bias_rows = const.tile([P, P], BF16)
         nc.gpsimd.memset(bias_rows[:], 0.0)
+        w_scales = const.tile([P, 3 * C], U8, align_bytes=64)
+        nc.gpsimd.memset(w_scales[:].bitcast(F32), 0.0)
+        warm_in = const.tile([P, 1], F32)
+        nc.gpsimd.memset(warm_in[:], 1.0)
 
         x_sb = const.tile([P, B, C], BF16)
-        for b in range(B):
-            nc.sync.dma_start(out=x_sb[:, b, :], in_=x[b])
+        nc.sync.dma_start(out=x_sb[:], in_=x.rearrange("b l c -> l b c"))
         w_words = const.tile([P, 2 * 3 * C], U8, align_bytes=64)
         nc.sync.dma_start(out=w_words[:].bitcast(I32), in_=W_qkv_words[0].bitcast(I32))
         for quad in range(4):
@@ -59,14 +61,14 @@ def tile_selfattention_pa_s_kernel(
                 in_=W_qkv_scales[0, 4 * quad : 4 * quad + 4, :].bitcast(I32),
             )
 
-        log_mul_all = const.tile([P, H], BF16)
-        nc.scalar.dma_start(
-            out=log_mul_all[:],
-            in_=log_scale_mul.rearrange("o h p q -> (o h p q)").partition_broadcast(P),
-        )
         nc.scalar.dma_start(out=bias_rows[0:TILES, :], in_=q_bias.rearrange("(f n) -> f n", n=P))
         nc.scalar.dma_start(
             out=bias_rows[TILES : 2 * TILES, :], in_=v_bias.rearrange("(f n) -> f n", n=P)
+        )
+        log_mul_all = const.tile([P, H], BF16)
+        nc.sync.dma_start(
+            out=log_mul_all[:],
+            in_=log_scale_mul.rearrange("o h p q -> (o h p q)").partition_broadcast(P),
         )
 
         ident = const.tile([P, P], F32)
@@ -74,20 +76,27 @@ def tile_selfattention_pa_s_kernel(
         ident_bf16 = const.tile([P, P], BF16)
         make_identity(nc, ident_bf16[:])
 
-        mul_all = const.tile([P, H], F32)
-        nc.scalar.activation(out=mul_all[:], in_=log_mul_all[:], func=ACT.Exp)
-        table_warm = const.tile([P, H], F32)
-        nc.scalar.activation(out=table_warm[:], in_=mul_all[:], func=ACT.Abs_reciprocal_sqrt)
+        table_warm = const.tile([P, 1], F32)
+        nc.scalar.activation(out=table_warm[:], in_=warm_in[:], func=ACT.Abs_reciprocal_sqrt)
         floor = const.tile([P, 1], F32)
         nc.gpsimd.memset(floor[:], EPS * EPS)
         neg_floor = const.tile([P, 1], F32)
         nc.gpsimd.memset(neg_floor[:], -EPS * EPS)
-        scale_mul = const.tile([P, TILES], F32)
+        two = const.tile([P, TILES], F32)
+        nc.gpsimd.memset(two[:], 2.0)
+        log2_mul = const.tile([P, TILES], F32)
         for i in range(HEADS_PER_TILE):
             rows = slice(D * i, D * (i + 1))
-            nc.gpsimd.tensor_scalar_min(
-                out=scale_mul[rows, :], in0=mul_all[rows, i:H:HEADS_PER_TILE], scalar1=MAX_MUL
+            nc.gpsimd.tensor_scalar(
+                out=log2_mul[rows, :],
+                in0=log_mul_all[rows, i:H:HEADS_PER_TILE],
+                scalar1=math.log(MAX_MUL),
+                scalar2=1.0 / math.log(2.0),
+                op0=ALU.min,
+                op1=ALU.mult,
             )
+        scale_mul = const.tile([P, TILES], F32)
+        nc.gpsimd.tensor_tensor(out=scale_mul[:], in0=two[:], in1=log2_mul[:], op=ALU.pow)
 
         grouped = const.tile([P, B, L * PACK], BF16, align_bytes=64)
         x_codes = const.tile([P, B, L], U32, align_bytes=64)

@@ -98,6 +98,14 @@ def tile_selfattention_pa_s_kernel(
         scale_mul = const.tile([P, TILES], F32)
         nc.gpsimd.tensor_tensor(out=scale_mul[:], in0=two[:], in1=log2_mul[:], op=ALU.pow)
 
+        idle_operand = const.tile([P, C], BF16)
+        nc.vector.memset(idle_operand[:], 0.0)
+        idle_out = acc_pool.tile([P, C], F32, name="acc")
+        for repeat in range(2):
+            nc.tensor.matmul(
+                out=idle_out[:], lhsT=idle_operand[:, 0:P], rhs=idle_operand[:], start=True, stop=True
+            )
+
         grouped = const.tile([P, B, L * PACK], BF16, align_bytes=64)
         x_codes = const.tile([P, B, L], U32, align_bytes=64)
         x_scales = const.tile([P, B, L], U8, align_bytes=64)
@@ -185,30 +193,32 @@ def tile_selfattention_pa_s_kernel(
             )
             factor[part, b] = inv_norm
 
-        def scale(part, b):
+        def scale_and_store(part, b, pieces):
             if part == "q":
                 nc.vector.tensor_mul(
                     out=factor[part, b][:],
                     in0=factor[part, b][:],
                     in1=scale_mul[:].unsqueeze(2).to_broadcast([P, TILES, RUN]),
                 )
-            scaled = work.tile([P, SEGS, D], F32)
-            nc.vector.tensor_mul(
-                out=scaled[:],
-                in0=heads[part, b][:],
-                in1=factor[part, b][:]
-                .rearrange("p f j -> p (f j)")
-                .unsqueeze(2)
-                .to_broadcast([P, SEGS, D]),
-            )
-            heads[part, b] = scaled
+            scaled = work.tile([P, TILES, RUN, D], F32)
+            unscaled = heads[part, b][:].rearrange("p (f j) d -> p f j d", j=RUN)
+            width = TILES // pieces
+            for f0 in range(0, TILES, width):
+                nc.vector.tensor_mul(
+                    out=scaled[:, f0 : f0 + width],
+                    in0=unscaled[:, f0 : f0 + width],
+                    in1=factor[part, b][:, f0 : f0 + width, :]
+                    .unsqueeze(3)
+                    .to_broadcast([P, width, RUN, D]),
+                )
+                store(part, b, scaled, f0, width)
 
-        def store(part, b):
+        def store(part, b, tile, f0, width):
             nc.sync.dma_start(
                 out=outputs[part][b].rearrange(
                     "(f i) (a j) d -> (i a) f (j d)", i=HEADS_PER_TILE, j=RUN
-                ),
-                in_=heads[part, b][:].rearrange("p (f j) d -> p f (j d)", j=RUN),
+                )[:, f0 : f0 + width, :],
+                in_=tile[:, f0 : f0 + width].rearrange("p f j d -> p f (j d)"),
             )
 
         for b in range(B):
@@ -227,11 +237,10 @@ def tile_selfattention_pa_s_kernel(
             sum_squares("k", b)
             sum_squares("q", b)
             turn("v", b)
-            store("v", b)
+            store("v", b, heads["v", b][:].rearrange("p (f j) d -> p f j d", j=RUN), 0, TILES)
         for b in range(B):
             inverse_norm("k", b)
             inverse_norm("q", b)
         for b in range(B):
             for part in ("k", "q"):
-                scale(part, b)
-                store(part, b)
+                scale_and_store(part, b, 2 if (part, b) == ("q", B - 1) else 1)

@@ -118,6 +118,7 @@ def tile_selfattention_pa_s_kernel(
                 out=grouped[:, b, :].bitcast(F32).rearrange("p (j a u) -> p j a u", j=RUN, u=2),
                 in_=xt[:].rearrange("p u (a j) -> p j a u", j=RUN),
             )
+        for b in range(B):
             nc.vector.quantize_mx(
                 out=x_codes[:, b, :].bitcast(FP8X4), scales=x_scales[:, b, :], in_=grouped[:, b, :]
             )
@@ -178,28 +179,34 @@ def tile_selfattention_pa_s_kernel(
             nc.vector.tensor_reduce(out=sumsq[:], in_=squares[part, b][:], axis=AX.X, op=ALU.add)
             squares[part, b] = sumsq
 
-        def inverse_norm(part, b):
+        excesses = {}
+
+        def clamp(part, b):
             excess = work.tile([P, SEGS], F32)
             nc.scalar.activation(
                 out=excess[:], in_=squares[part, b][:], func=ACT.Relu, bias=neg_floor[:], scale=1.0
             )
+            excesses[part, b] = excess
+
+        def inverse_norm(part, b):
             inv_norm = work.tile([P, TILES, RUN], F32)
             nc.scalar.activation(
                 out=inv_norm[:].rearrange("p f j -> p (f j)"),
-                in_=excess[:],
+                in_=excesses[part, b][:],
                 func=ACT.Abs_reciprocal_sqrt,
                 bias=floor[:],
                 scale=1.0,
             )
             factor[part, b] = inv_norm
 
+        def times_multiplier(b):
+            nc.vector.tensor_mul(
+                out=factor["q", b][:],
+                in0=factor["q", b][:],
+                in1=scale_mul[:].unsqueeze(2).to_broadcast([P, TILES, RUN]),
+            )
+
         def scale_and_store(part, b, pieces):
-            if part == "q":
-                nc.vector.tensor_mul(
-                    out=factor[part, b][:],
-                    in0=factor[part, b][:],
-                    in1=scale_mul[:].unsqueeze(2).to_broadcast([P, TILES, RUN]),
-                )
             scaled = work.tile([P, TILES, RUN, D], F32)
             unscaled = heads[part, b][:].rearrange("p (f j) d -> p f j d", j=RUN)
             width = TILES // pieces
@@ -239,8 +246,11 @@ def tile_selfattention_pa_s_kernel(
             turn("v", b)
             store("v", b, heads["v", b][:].rearrange("p (f j) d -> p f j d", j=RUN), 0, TILES)
         for b in range(B):
-            inverse_norm("k", b)
-            inverse_norm("q", b)
+            for part in ("q", "k"):
+                clamp(part, b)
+            for part in ("q", "k"):
+                inverse_norm(part, b)
         for b in range(B):
-            for part in ("k", "q"):
-                scale_and_store(part, b, 2 if (part, b) == ("q", B - 1) else 1)
+            times_multiplier(b)
+            scale_and_store("k", b, 1)
+            scale_and_store("q", b, b + 1)

@@ -118,7 +118,6 @@ def tile_selfattention_pa_s_kernel(
                 out=grouped[:, b, :].bitcast(F32).rearrange("p (j a u) -> p j a u", j=RUN, u=2),
                 in_=xt[:].rearrange("p u (a j) -> p j a u", j=RUN),
             )
-        for b in range(B):
             nc.vector.quantize_mx(
                 out=x_codes[:, b, :].bitcast(FP8X4), scales=x_scales[:, b, :], in_=grouped[:, b, :]
             )

@@ -114,7 +114,7 @@ def tile_selfattention_pa_s_kernel(
             xt = xt_pool.tile([P, 2, L], F32)
             for u in range(2):
                 nc.tensor.transpose(xt[:, u, :], x_words[:, u : C // 2 : 2], ident[:])
-            nc.vector.tensor_copy(
+            nc.scalar.copy(
                 out=grouped[:, b, :].bitcast(F32).rearrange("p (j a u) -> p j a u", j=RUN, u=2),
                 in_=xt[:].rearrange("p u (a j) -> p j a u", j=RUN),
             )

@@ -147,6 +147,9 @@ def tile_selfattention_pa_s_kernel(
                 )
             raw[part, b] = acc
 
+        def store_v(b):
+            store("v", b, heads["v", b][:].rearrange("p (f j) d -> p f j d", j=RUN), 0, TILES)
+
         def add_bias(part, b):
             biased = work.tile([P, TILES, L], F32, align_bytes=64)
             for f in range(TILES):
@@ -227,29 +230,43 @@ def tile_selfattention_pa_s_kernel(
                 in_=tile[:, f0 : f0 + width].rearrange("p f j d -> p f (j d)"),
             )
 
+        project("k", 0)
+        project("v", 0)
+        project("k", 1)
+        project("q", 0)
+        project("v", 1)
+        project("q", 1)
+        turn("k", 0)
+        add_bias("v", 0)
+        turn("k", 1)
+        square("k", 0)
+        add_bias("q", 0)
+        turn("v", 0)
+        store_v(0)
+        square("k", 1)
+        add_bias("q", 1)
+        sum_squares("k", 0)
+        turn("q", 0)
+        sum_squares("k", 1)
+        square("q", 0)
+        turn("q", 1)
         for b in range(B):
-            project("q", b)
-            add_bias("q", b)
-            project("k", b)
+            clamp("k", b)
         for b in range(B):
-            turn("k", b)
-            turn("q", b)
-        for b in range(B):
-            project("v", b)
-            square("k", b)
-            square("q", b)
-            add_bias("v", b)
-        for b in range(B):
-            sum_squares("k", b)
-            sum_squares("q", b)
-            turn("v", b)
-            store("v", b, heads["v", b][:].rearrange("p (f j) d -> p f j d", j=RUN), 0, TILES)
-        for b in range(B):
-            for part in ("q", "k"):
-                clamp(part, b)
-            for part in ("q", "k"):
-                inverse_norm(part, b)
-        for b in range(B):
-            times_multiplier(b)
-            scale_and_store("k", b, 1)
-            scale_and_store("q", b, b + 1)
+            inverse_norm("k", b)
+        add_bias("v", 1)
+        square("q", 1)
+        sum_squares("q", 0)
+        scale_and_store("k", 0, 1)
+        clamp("q", 0)
+        inverse_norm("q", 0)
+        turn("v", 1)
+        store_v(1)
+        sum_squares("q", 1)
+        scale_and_store("k", 1, 1)
+        times_multiplier(0)
+        clamp("q", 1)
+        inverse_norm("q", 1)
+        scale_and_store("q", 0, 1)
+        times_multiplier(1)
+        scale_and_store("q", 1, 2)

@@ -24,6 +24,8 @@ RUN = L // D
 SEGS = TILES * RUN
 MAX_MUL = 100.0
 EPS = 1e-12
+IDLE_BEFORE_X = 400
+IDLE_BEFORE_CODES = 192
 
 FLOPS = 2 * B * L * C * 3 * C
 
@@ -98,13 +100,20 @@ def tile_selfattention_pa_s_kernel(
         scale_mul = const.tile([P, TILES], F32)
         nc.gpsimd.tensor_tensor(out=scale_mul[:], in0=two[:], in1=log2_mul[:], op=ALU.pow)
 
-        idle_operand = const.tile([P, C], BF16)
+        idle_operand = const.tile([P, P], F32)
         nc.vector.memset(idle_operand[:], 0.0)
         idle_out = acc_pool.tile([P, C], F32, name="acc")
-        for repeat in range(2):
+
+        def idle_matmul(columns):
             nc.tensor.matmul(
-                out=idle_out[:], lhsT=idle_operand[:, 0:P], rhs=idle_operand[:], start=True, stop=True
+                out=idle_out[:, 0:columns],
+                lhsT=idle_operand[:],
+                rhs=idle_operand[:, 0:1].to_broadcast([P, columns]),
+                start=True,
+                stop=True,
             )
+
+        idle_matmul(IDLE_BEFORE_X)
 
         grouped = const.tile([P, B, L * PACK], BF16, align_bytes=64)
         x_codes = const.tile([P, B, L], U32, align_bytes=64)
@@ -124,6 +133,7 @@ def tile_selfattention_pa_s_kernel(
 
         bias_t = bias_pool.tile([P, P], BF16)
         nc.tensor.transpose(bias_t[:], bias_rows[:], ident_bf16[:])
+        idle_matmul(IDLE_BEFORE_CODES)
         bias_col = const.tile([P, 2 * TILES], F32)
         nc.vector.tensor_copy(out=bias_col[:], in_=bias_t[:, 0 : 2 * TILES])
 

@@ -24,8 +24,9 @@ RUN = L // D
 SEGS = TILES * RUN
 MAX_MUL = 100.0
 EPS = 1e-12
-IDLE_BEFORE_X = 400
-IDLE_BEFORE_CODES = 192
+IDLE_FIRST = 384
+IDLE_BEFORE_X = 220
+IDLE_BEFORE_CODES = 128
 
 FLOPS = 2 * B * L * C * 3 * C
 
@@ -100,20 +101,23 @@ def tile_selfattention_pa_s_kernel(
         scale_mul = const.tile([P, TILES], F32)
         nc.gpsimd.tensor_tensor(out=scale_mul[:], in0=two[:], in1=log2_mul[:], op=ALU.pow)
 
+        idle_bf16 = const.tile([P, P], BF16)
+        nc.vector.memset(idle_bf16[:], 0.0)
         idle_operand = const.tile([P, P], F32)
         nc.vector.memset(idle_operand[:], 0.0)
         idle_out = acc_pool.tile([P, C], F32, name="acc")
 
-        def idle_matmul(columns):
+        def idle_matmul(operand, columns):
             nc.tensor.matmul(
                 out=idle_out[:, 0:columns],
-                lhsT=idle_operand[:],
-                rhs=idle_operand[:, 0:1].to_broadcast([P, columns]),
+                lhsT=operand[:],
+                rhs=operand[:, 0:1].to_broadcast([P, columns]),
                 start=True,
                 stop=True,
             )
 
-        idle_matmul(IDLE_BEFORE_X)
+        idle_matmul(idle_bf16, IDLE_FIRST)
+        idle_matmul(idle_operand, IDLE_BEFORE_X)
 
         grouped = const.tile([P, B, L * PACK], BF16, align_bytes=64)
         x_codes = const.tile([P, B, L], U32, align_bytes=64)
@@ -133,7 +137,7 @@ def tile_selfattention_pa_s_kernel(
 
         bias_t = bias_pool.tile([P, P], BF16)
         nc.tensor.transpose(bias_t[:], bias_rows[:], ident_bf16[:])
-        idle_matmul(IDLE_BEFORE_CODES)
+        idle_matmul(idle_operand, IDLE_BEFORE_CODES)
         bias_col = const.tile([P, 2 * TILES], F32)
         nc.vector.tensor_copy(out=bias_col[:], in_=bias_t[:, 0 : 2 * TILES])
 
@@ -218,19 +222,29 @@ def tile_selfattention_pa_s_kernel(
                 in1=scale_mul[:].unsqueeze(2).to_broadcast([P, TILES, RUN]),
             )
 
+        scaled_tiles = {}
+
+        def scale(part, b, f0, width):
+            if (part, b) not in scaled_tiles:
+                scaled = work.tile([P, TILES, RUN, D], F32)
+                scaled_tiles[part, b] = scaled
+            tile = scaled_tiles[part, b]
+            nc.vector.tensor_mul(
+                out=tile[:, f0 : f0 + width],
+                in0=heads[part, b][:].rearrange("p (f j) d -> p f j d", j=RUN)[:, f0 : f0 + width],
+                in1=factor[part, b][:, f0 : f0 + width, :]
+                .unsqueeze(3)
+                .to_broadcast([P, width, RUN, D]),
+            )
+
+        def store_scaled(part, b, f0, width):
+            store(part, b, scaled_tiles[part, b], f0, width)
+
         def scale_and_store(part, b, pieces):
-            scaled = work.tile([P, TILES, RUN, D], F32)
-            unscaled = heads[part, b][:].rearrange("p (f j) d -> p f j d", j=RUN)
             width = TILES // pieces
             for f0 in range(0, TILES, width):
-                nc.vector.tensor_mul(
-                    out=scaled[:, f0 : f0 + width],
-                    in0=unscaled[:, f0 : f0 + width],
-                    in1=factor[part, b][:, f0 : f0 + width, :]
-                    .unsqueeze(3)
-                    .to_broadcast([P, width, RUN, D]),
-                )
-                store(part, b, scaled, f0, width)
+                scale(part, b, f0, width)
+                store_scaled(part, b, f0, width)
 
         def store(part, b, tile, f0, width):
             nc.sync.dma_start(
@@ -273,10 +287,12 @@ def tile_selfattention_pa_s_kernel(
         turn("v", 1)
         store_v(1)
         sum_squares("q", 1)
-        scale_and_store("k", 1, 1)
         times_multiplier(0)
+        scale_and_store("k", 1, 1)
         clamp("q", 1)
         inverse_norm("q", 1)
-        scale_and_store("q", 0, 1)
+        scale("q", 0, 0, 2)
         times_multiplier(1)
+        scale("q", 0, 2, 2)
+        store_scaled("q", 0, 0, TILES)
         scale_and_store("q", 1, 2)

@@ -24,7 +24,7 @@ RUN = L // D
 SEGS = TILES * RUN
 MAX_MUL = 100.0
 EPS = 1e-12
-IDLE_FIRST = 384
+IDLE_FIRST = 512
 IDLE_BEFORE_X = 220
 IDLE_BEFORE_CODES = 128
 

import math
from contextlib import ExitStack

import concourse.mybir as mybir
from concourse.masks import make_identity

F32 = mybir.dt.float32
BF16 = mybir.dt.bfloat16
I32 = mybir.dt.int32
U32 = mybir.dt.uint32
U8 = mybir.dt.uint8
FP8X4 = mybir.dt.float8_e4m3fn_x4
FP4X4 = mybir.dt.float4_e2m1fn_x4
ACT = mybir.ActivationFunctionType
ALU = mybir.AluOpType
AX = mybir.AxisListType

P = 128
B, L, C, H, D = 2, 128, 512, 16, 32
PACK = 4
TILES = C // P
HEADS_PER_TILE = P // D
RUN = L // D
SEGS = TILES * RUN
MAX_MUL = 100.0
EPS = 1e-12
IDLE_FIRST = 512
IDLE_BEFORE_X = 220
IDLE_BEFORE_CODES = 128

FLOPS = 2 * B * L * C * 3 * C


def tile_selfattention_pa_s_kernel(
    tc, x, W_qkv_words, W_qkv_scales, q_bias, v_bias, log_scale_mul, out_0, out_1, out_2
):
    nc = tc.nc
    outputs = {"q": out_0, "k": out_1, "v": out_2}
    first_tile = {"q": 0, "k": TILES, "v": 2 * TILES}
    bias_column = {"q": 0, "v": TILES}

    with ExitStack() as ctx:
        const = ctx.enter_context(tc.tile_pool(name="const", bufs=1))
        work = ctx.enter_context(tc.tile_pool(name="work", bufs=6))
        xt_pool = ctx.enter_context(tc.psum_pool(name="xt_pool", bufs=2))
        bias_pool = ctx.enter_context(tc.psum_pool(name="bias_pool", bufs=1))
        acc_pool = ctx.enter_context(tc.psum_pool(name="acc_pool", bufs=5))
        ctx.enter_context(tc.manual_schedule())

        bias_rows = const.tile([P, P], BF16)
        nc.gpsimd.memset(bias_rows[:], 0.0)
        w_scales = const.tile([P, 3 * C], U8, align_bytes=64)
        nc.gpsimd.memset(w_scales[:].bitcast(F32), 0.0)
        warm_in = const.tile([P, 1], F32)
        nc.gpsimd.memset(warm_in[:], 1.0)

        x_sb = const.tile([P, B, C], BF16)
        nc.sync.dma_start(out=x_sb[:], in_=x.rearrange("b l c -> l b c"))
        w_words = const.tile([P, 2 * 3 * C], U8, align_bytes=64)
        nc.sync.dma_start(out=w_words[:].bitcast(I32), in_=W_qkv_words[0].bitcast(I32))
        for quad in range(4):
            nc.sync.dma_start(
                out=w_scales[32 * quad : 32 * quad + 4, :].bitcast(I32),
                in_=W_qkv_scales[0, 4 * quad : 4 * quad + 4, :].bitcast(I32),
            )

        nc.scalar.dma_start(out=bias_rows[0:TILES, :], in_=q_bias.rearrange("(f n) -> f n", n=P))
        nc.scalar.dma_start(
            out=bias_rows[TILES : 2 * TILES, :], in_=v_bias.rearrange("(f n) -> f n", n=P)
        )
        log_mul_all = const.tile([P, H], BF16)
        nc.sync.dma_start(
            out=log_mul_all[:],
            in_=log_scale_mul.rearrange("o h p q -> (o h p q)").partition_broadcast(P),
        )

        ident = const.tile([P, P], F32)
        make_identity(nc, ident[:])
        ident_bf16 = const.tile([P, P], BF16)
        make_identity(nc, ident_bf16[:])

        table_warm = const.tile([P, 1], F32)
        nc.scalar.activation(out=table_warm[:], in_=warm_in[:], func=ACT.Abs_reciprocal_sqrt)
        floor = const.tile([P, 1], F32)
        nc.gpsimd.memset(floor[:], EPS * EPS)
        neg_floor = const.tile([P, 1], F32)
        nc.gpsimd.memset(neg_floor[:], -EPS * EPS)
        two = const.tile([P, TILES], F32)
        nc.gpsimd.memset(two[:], 2.0)
        log2_mul = const.tile([P, TILES], F32)
        for i in range(HEADS_PER_TILE):
            rows = slice(D * i, D * (i + 1))
            nc.gpsimd.tensor_scalar(
                out=log2_mul[rows, :],
                in0=log_mul_all[rows, i:H:HEADS_PER_TILE],
                scalar1=math.log(MAX_MUL),
                scalar2=1.0 / math.log(2.0),
                op0=ALU.min,
                op1=ALU.mult,
            )
        scale_mul = const.tile([P, TILES], F32)
        nc.gpsimd.tensor_tensor(out=scale_mul[:], in0=two[:], in1=log2_mul[:], op=ALU.pow)

        idle_bf16 = const.tile([P, P], BF16)
        nc.vector.memset(idle_bf16[:], 0.0)
        idle_operand = const.tile([P, P], F32)
        nc.vector.memset(idle_operand[:], 0.0)
        idle_out = acc_pool.tile([P, C], F32, name="acc")

        def idle_matmul(operand, columns):
            nc.tensor.matmul(
                out=idle_out[:, 0:columns],
                lhsT=operand[:],
                rhs=operand[:, 0:1].to_broadcast([P, columns]),
                start=True,
                stop=True,
            )

        idle_matmul(idle_bf16, IDLE_FIRST)
        idle_matmul(idle_operand, IDLE_BEFORE_X)

        grouped = const.tile([P, B, L * PACK], BF16, align_bytes=64)
        x_codes = const.tile([P, B, L], U32, align_bytes=64)
        x_scales = const.tile([P, B, L], U8, align_bytes=64)
        for b in range(B):
            x_words = x_sb[:, b, :].bitcast(F32)
            xt = xt_pool.tile([P, 2, L], F32)
            for u in range(2):
                nc.tensor.transpose(xt[:, u, :], x_words[:, u : C // 2 : 2], ident[:])
            nc.scalar.copy(
                out=grouped[:, b, :].bitcast(F32).rearrange("p (j a u) -> p j a u", j=RUN, u=2),
                in_=xt[:].rearrange("p u (a j) -> p j a u", j=RUN),
            )
            nc.vector.quantize_mx(
                out=x_codes[:, b, :].bitcast(FP8X4), scales=x_scales[:, b, :], in_=grouped[:, b, :]
            )

        bias_t = bias_pool.tile([P, P], BF16)
        nc.tensor.transpose(bias_t[:], bias_rows[:], ident_bf16[:])
        idle_matmul(idle_operand, IDLE_BEFORE_CODES)
        bias_col = const.tile([P, 2 * TILES], F32)
        nc.vector.tensor_copy(out=bias_col[:], in_=bias_t[:, 0 : 2 * TILES])

        raw = {}
        heads = {}
        squares = {}
        factor = {}

        def project(part, b):
            acc = acc_pool.tile([P, TILES, L], F32)
            for f in range(TILES):
                t = first_tile[part] + f
                nc.tensor.matmul_mx(
                    out=acc[:, f, :],
                    lhsT=w_words[:, 2 * P * t : 2 * P * (t + 1)].bitcast(FP4X4),
                    lhsT_scale=w_scales[:, P * t : P * (t + 1)],
                    rhs=x_codes[:, b, :].bitcast(FP8X4),
                    rhs_scale=x_scales[:, b, :],
                    start=True,
                    stop=True,
                )
            raw[part, b] = acc

        def store_v(b):
            store("v", b, heads["v", b][:].rearrange("p (f j) d -> p f j d", j=RUN), 0, TILES)

        def add_bias(part, b):
            biased = work.tile([P, TILES, L], F32, align_bytes=64)
            for f in range(TILES):
                column = bias_column[part] + f
                nc.scalar.activation(
                    out=biased[:, f, :],
                    in_=raw[part, b][:, f, :],
                    func=ACT.Identity,
                    bias=bias_col[:, column : column + 1],
                    scale=1.0,
                )
            raw[part, b] = biased

        def turn(part, b):
            turned = work.tile([P, SEGS, D], F32, align_bytes=64)
            nc.vector.transpose(
                out=turned[:].rearrange("p s d -> p (s d)"),
                in_=raw[part, b][:].rearrange("p f n -> p (f n)"),
            )
            heads[part, b] = turned

        def square(part, b):
            squared = work.tile([P, SEGS, D], F32)
            nc.scalar.activation(out=squared[:], in_=heads[part, b][:], func=ACT.Square)
            squares[part, b] = squared

        def sum_squares(part, b):
            sumsq = work.tile([P, SEGS], F32)
            nc.vector.tensor_reduce(out=sumsq[:], in_=squares[part, b][:], axis=AX.X, op=ALU.add)
            squares[part, b] = sumsq

        excesses = {}

        def clamp(part, b):
            excess = work.tile([P, SEGS], F32)
            nc.scalar.activation(
                out=excess[:], in_=squares[part, b][:], func=ACT.Relu, bias=neg_floor[:], scale=1.0
            )
            excesses[part, b] = excess

        def inverse_norm(part, b):
            inv_norm = work.tile([P, TILES, RUN], F32)
            nc.scalar.activation(
                out=inv_norm[:].rearrange("p f j -> p (f j)"),
                in_=excesses[part, b][:],
                func=ACT.Abs_reciprocal_sqrt,
                bias=floor[:],
                scale=1.0,
            )
            factor[part, b] = inv_norm

        def times_multiplier(b):
            nc.vector.tensor_mul(
                out=factor["q", b][:],
                in0=factor["q", b][:],
                in1=scale_mul[:].unsqueeze(2).to_broadcast([P, TILES, RUN]),
            )

        scaled_tiles = {}

        def scale(part, b, f0, width):
            if (part, b) not in scaled_tiles:
                scaled = work.tile([P, TILES, RUN, D], F32)
                scaled_tiles[part, b] = scaled
            tile = scaled_tiles[part, b]
            nc.vector.tensor_mul(
                out=tile[:, f0 : f0 + width],
                in0=heads[part, b][:].rearrange("p (f j) d -> p f j d", j=RUN)[:, f0 : f0 + width],
                in1=factor[part, b][:, f0 : f0 + width, :]
                .unsqueeze(3)
                .to_broadcast([P, width, RUN, D]),
            )

        def store_scaled(part, b, f0, width):
            store(part, b, scaled_tiles[part, b], f0, width)

        def scale_and_store(part, b, pieces):
            width = TILES // pieces
            for f0 in range(0, TILES, width):
                scale(part, b, f0, width)
                store_scaled(part, b, f0, width)

        def store(part, b, tile, f0, width):
            nc.sync.dma_start(
                out=outputs[part][b].rearrange(
                    "(f i) (a j) d -> (i a) f (j d)", i=HEADS_PER_TILE, j=RUN
                )[:, f0 : f0 + width, :],
                in_=tile[:, f0 : f0 + width].rearrange("p f j d -> p f (j d)"),
            )

        project("k", 0)
        project("v", 0)
        project("k", 1)
        project("q", 0)
        project("v", 1)
        project("q", 1)
        turn("k", 0)
        add_bias("v", 0)
        turn("k", 1)
        square("k", 0)
        add_bias("q", 0)
        turn("v", 0)
        store_v(0)
        square("k", 1)
        add_bias("q", 1)
        sum_squares("k", 0)
        turn("q", 0)
        sum_squares("k", 1)
        square("q", 0)
        turn("q", 1)
        for b in range(B):
            clamp("k", b)
        for b in range(B):
            inverse_norm("k", b)
        add_bias("v", 1)
        square("q", 1)
        sum_squares("q", 0)
        scale_and_store("k", 0, 1)
        clamp("q", 0)
        inverse_norm("q", 0)
        turn("v", 1)
        store_v(1)
        sum_squares("q", 1)
        times_multiplier(0)
        scale_and_store("k", 1, 1)
        clamp("q", 1)
        inverse_norm("q", 1)
        scale("q", 0, 0, 2)
        times_multiplier(1)
        scale("q", 0, 2, 2)
        store_scaled("q", 0, 0, TILES)
        scale_and_store("q", 1, 2)
